import numpy as np
import ml_dtypes


def mxq(x, axis, fmt="e4m3"):
    dtype, down = {"e4m3": (ml_dtypes.float8_e4m3fn, 7), "e5m2": (ml_dtypes.float8_e5m2, 14)}[fmt]
    v = np.moveaxis(np.asarray(x, np.float32).astype(ml_dtypes.bfloat16).astype(np.float64), axis, -1)
    blocks = v.reshape(v.shape[:-1] + (-1, 32))
    amax = np.abs(blocks).max(-1, keepdims=True)
    byte = np.maximum(np.where(amax > 0, np.frexp(amax)[1] - 1 + 127, 0) - down, 1)
    scale = np.exp2(byte - 127.0)
    codes = (blocks / scale).astype(np.float32).astype(dtype).astype(np.float64)
    return np.moveaxis((codes * scale).reshape(v.shape), -1, axis)


WIDE = False


def mx_kscale(k):
    if not WIDE:
        return np.ones(k)
    levels = np.array([10, -10, 5, -5, 0])
    if k % 512:
        return np.exp2(np.random.permutation(np.resize(levels, k // 32))).repeat(32)
    a = np.empty((k // 512, 16))
    for p in range(k // 512):
        a[p, :8] = np.random.permutation(np.resize(levels, 8))
        for g in range(8):
            far = levels[np.abs(levels - a[p, g]) >= 10]
            a[p, g + 8] = far[np.random.randint(len(far))]
    return np.exp2(a.ravel()).repeat(32)


BF16 = ml_dtypes.bfloat16


def bf(x):
    return np.asarray(x, np.float32).astype(BF16)


def f64(x):
    return np.asarray(x).astype(np.float64)


B, T, D, F = 4, 128, 1024, 1024
K2, K3, K4 = 2, 3, 4
EPS = 1e-12


def conv_branch(xq, w, b):
    kw = w.shape[1]
    n = xq.shape[1] - kw + 1
    wq = mxq(f64(w), 2, "e4m3")
    out = sum((xq[:, k:k + n, :] @ wq[:, k, :].T) for k in range(kw))
    return np.maximum(out + f64(b), 0.0)


def l2norm(x, axis):
    n = np.sqrt(np.sum(x * x, axis=axis, keepdims=True))
    return x / np.maximum(n, EPS)


def setup_inputs():
    s = mx_kscale(D)
    return {"words_emb": bf(np.random.standard_normal((B, T, D)) * s),
            "W2": bf(np.random.standard_normal((F, K2, D)) / np.sqrt(K2 * D) / s), "b2": bf(np.random.standard_normal(F) * 0.3),
            "W3": bf(np.random.standard_normal((F, K3, D)) / np.sqrt(K3 * D) / s), "b3": bf(np.random.standard_normal(F) * 0.3),
            "W4": bf(np.random.standard_normal((F, K4, D)) / np.sqrt(K4 * D) / s), "b4": bf(np.random.standard_normal(F) * 0.3)}


def reference(words_emb, W2, b2, W3, b3, W4, b4):
    xq = mxq(f64(words_emb), 2, "e4m3")
    a = conv_branch(xq, W2, b2)
    b_ = conv_branch(xq, W3, b3)
    c = conv_branch(xq, W4, b4)
    seq = T - K4 + 1
    main = np.maximum(np.maximum(a[:, :seq], b_[:, :seq]), c[:, :seq])
    pen = np.maximum(a[:, seq], b_[:, seq])[:, None]
    last = a[:, seq + 1][:, None]
    code = np.concatenate([main, pen, last], axis=1)
    code = l2norm(code, 2)
    return code.transpose(0, 2, 1)

@@ -1,0 +1,352 @@
+from contextlib import ExitStack
+
+import concourse.mybir as mybir
+from concourse.masks import make_identity
+
+F32 = mybir.dt.float32
+BF16 = mybir.dt.bfloat16
+U32 = mybir.dt.uint32
+U8 = mybir.dt.uint8
+FP8X4 = mybir.dt.float8_e4m3fn_x4
+ACT = mybir.ActivationFunctionType
+ALU = mybir.AluOpType
+
+P = 128
+B = 4
+T = 128
+D = 1024
+F = 1024
+NI = F // P
+WIDTHS = (2, 3, 4)
+R = 4
+NPL = R + 3
+HC = NPL * 64
+FLOPS = 2 * B * (127 * 2 + 126 * 3 + 125 * 4) * D * F
+MANUAL = True
+LAST = 1
+ALT = "VSVSVSVS"
+FULL = (0, 4)
+HALF = ((0, 2), (2, 2))
+QCALLS = {2: ((0, 2048),), 3: ((0, 2048), (2048, 1024)), 4: ((0, 4096),)}
+
+
+def tile_textheading_pa_kernel(tc, words_emb, W2, b2, W3, b3, W4, b4, out):
+    nc = tc.nc
+    Wd = {2: W2, 3: W3, 4: W4}
+    bd = {2: b2, 3: b3, 4: b4}
+    with ExitStack() as ctx:
+        if MANUAL:
+            ctx.enter_context(tc.manual_schedule())
+        const = ctx.enter_context(tc.tile_pool(name="const", bufs=1))
+        wpool = ctx.enter_context(tc.tile_pool(name="wraw", bufs=3))
+        gpool = ctx.enter_context(tc.tile_pool(name="grp", bufs=3))
+        cpool = ctx.enter_context(tc.tile_pool(name="codes", bufs=3))
+        epool = ctx.enter_context(tc.tile_pool(name="epi", bufs=2))
+        tp = ctx.enter_context(tc.psum_pool(name="tp", bufs=5))
+        accp = ctx.enter_context(tc.psum_pool(name="acc", bufs=1))
+
+        ident = const.tile([P, P], F32, name="ident")
+        make_identity(nc, ident[:])
+        ones = const.tile([P, P], F32, name="ones")
+        nc.vector.memset(ones[:], 1.0)
+        braw = {}
+        for K in WIDTHS:
+            braw[K] = const.tile([P, NI], BF16, name="braw%d" % K)
+            nc.scalar.dma_start(out=braw[K][:], in_=bd[K].rearrange("(m i) -> m i", i=NI))
+        bias = const.tile([P, 3, NI], F32, name="bias")
+        warm = const.tile([P, 1], F32, name="warm")
+        nc.scalar.activation(out=warm[:], in_=ones[:, 0:1], func=ACT.Abs_reciprocal_sqrt)
+
+        x_sb = const.tile([P, B, D], BF16, name="x_sb")
+        Wv = {}
+        for K in WIDTHS:
+            Wv[K] = Wd[K].rearrange("(m i) k d -> i m (k d)", i=NI)
+        wraw = {}
+
+        def load_x(n):
+            nc.sync.dma_start(out=x_sb[:, n, :], in_=words_emb[n])
+
+        def load_w(i, K):
+            wraw[(i, K)] = wpool.tile([P, K * D], BF16, name="w%d" % K, tag="w%d" % K)
+            nc.sync.dma_start(out=wraw[(i, K)][:], in_=Wv[K][i])
+
+        load_x(0)
+        load_x(1)
+        load_w(0, 2)
+        load_x(2)
+        load_x(3)
+        load_w(0, 3)
+        load_w(0, 4)
+        for i in (1, 2):
+            for K in WIDTHS:
+                load_w(i, K)
+
+        def copy(eng, dst, src):
+            if eng == "V":
+                nc.vector.tensor_copy(out=dst, in_=src)
+            else:
+                nc.scalar.copy(out=dst, in_=src)
+
+        xgh = []
+        xgw = []
+        xch = []
+        xsh = []
+        for h in range(2):
+            xgh.append(const.tile([P, 2 * HC * 4], BF16, name="xgh%d" % h, align_bytes=64))
+            xgw.append(xgh[h][:].bitcast(F32).rearrange("p (g r n q u) -> p g r n q u", g=2, r=NPL, n=2, q=32, u=2))
+            xch.append(const.tile([P, 2, HC], U32, name="xch%d" % h, align_bytes=64))
+            xsh.append(const.tile([P, 2, HC], U8, name="xsh%d" % h, align_bytes=64))
+            for g in range(2):
+                nc.vector.memset(xgw[h][:, g, R:NPL, :, 31:32, :], 0.0)
+
+        def tx(n, eng):
+            xb = tp.tile([P, 2, 2, P], F32, name="xb", tag="tp")
+            xw = x_sb[:, n, :].bitcast(F32)
+            for g in range(2):
+                for u in range(2):
+                    nc.tensor.transpose(xb[:, g, u, :], xw[:, 256 * g + u:256 * (g + 1):2], ident[:])
+            for g in range(2):
+                copy(eng, xgw[n // 2][:, g, 0:R, n % 2, :, :], xb[:, g, :, :].rearrange("p u (q r) -> p r q u", r=R))
+
+        def shift(h):
+            for g in range(2):
+                nc.vector.tensor_copy(out=xgw[h][:, g, R:NPL, :, 0:31, :], in_=xgw[h][:, g, 0:3, :, 1:32, :])
+
+        def quant_h(h, pl0, npl):
+            c0 = pl0 * 64
+            w = npl * 64
+            for g in range(2):
+                a = (g * HC + c0) * 4
+                nc.vector.quantize_mx(out=xch[h][:, g, c0:c0 + w].bitcast(FP8X4), scales=xsh[h][:, g, c0:c0 + w],
+                                      in_=xgh[h][:, a:a + 4 * w])
+
+        grp = {}
+        cod = {}
+
+        def transposes(i, K, engs):
+            gr = gpool.tile([P, K * 1024], BF16, name="g%d" % K, tag="g%d" % K, align_bytes=64)
+            grp[(i, K)] = gr
+            gr_w = gr[:].bitcast(F32).rearrange("p (k g f u) -> p k g f u", k=K, g=2, f=P, u=2)
+            ww = wraw[(i, K)][:].bitcast(F32)
+            for k in range(K):
+                bank = tp.tile([P, 2, 2, P], F32, name="bank", tag="tp")
+                for g in range(2):
+                    for u in range(2):
+                        o = 512 * k + 256 * g
+                        nc.tensor.transpose(bank[:, g, u, :], ww[:, o + u:o + 256:2], ident[:])
+                copy(engs[k], gr_w[:, k], bank[:].rearrange("p g u f -> p g f u"))
+            if i + 3 < NI:
+                load_w(i + 3, K)
+
+        def quantise(i, K):
+            cw = cpool.tile([P, K * 256], U32, name="c%d" % K, tag="c%d" % K, align_bytes=64)
+            sc = cpool.tile([P, K * 256], U8, name="s%d" % K, tag="s%d" % K, align_bytes=64)
+            cod[(i, K)] = (cw, sc)
+            gr = grp[(i, K)]
+            for (a, w) in QCALLS[K]:
+                nc.vector.quantize_mx(out=cw[:, a // 4:(a + w) // 4].bitcast(FP8X4),
+                                      scales=sc[:, a // 4:(a + w) // 4], in_=gr[:, a:a + w])
+
+        Tn = const.tile([P, NI, B, T], F32, name="Tn")
+        ssum = const.tile([P, B, T], F32, name="ssum")
+        rinv = const.tile([P, B, T], F32, name="rinv")
+        O = const.tile([P, B, NI * (T - 1)], F32, name="O")
+        accs = {}
+        tmps = {}
+        sqs = {}
+        rbs = {}
+
+        def paired(i):
+            return i < NI - LAST
+
+        def products(i, K, h):
+            if paired(i):
+                if h == 0:
+                    acc = accp.tile([P, 512], F32, name="acc%d" % K, tag="acc%d" % K)
+                    accs[(i, K, 0)] = acc[:, 0:256]
+                    accs[(i, K, 1)] = acc[:, 256:512]
+            else:
+                acch = accp.tile([P, 256], F32, name="acc%d" % K, tag="acc%d" % K)
+                accs[(i, K, h)] = acch[:]
+            cw, sc = cod[(i, K)]
+            for k in range(K):
+                for g in range(2):
+                    j = (2 * k + g) * P
+                    nc.tensor.matmul_mx(out=accs[(i, K, h)], lhsT=cw[:, j:j + P].bitcast(FP8X4),
+                                        lhsT_scale=sc[:, j:j + P],
+                                        rhs=xch[h][:, g, 64 * k:64 * k + 256].bitcast(FP8X4),
+                                        rhs_scale=xsh[h][:, g, 64 * k:64 * k + 256],
+                                        start=(k == 0 and g == 0), stop=(k == K - 1 and g == 1))
+
+        def relu(i, K, h):
+            if K == 2:
+                dst = Tn[:, i, 2 * h:2 * h + 2, :]
+            elif paired(i):
+                if h == 0:
+                    tf = epool.tile([P, B, T], F32, name="t%d" % K, tag="t%d" % K)
+                    tmps[(i, K, 0, 4)] = tf[:]
+                    tmps[(i, K, 0, 2)] = tf[:, 0:2, :]
+                    tmps[(i, K, 2, 2)] = tf[:, 2:4, :]
+                dst = tmps[(i, K, 2 * h, 2)]
+            else:
+                th = epool.tile([P, 2, T], F32, name="t%d" % K, tag="t%d" % K)
+                tmps[(i, K, 2 * h, 2)] = th[:]
+                dst = th[:]
+            nc.scalar.activation(out=dst.rearrange("p n (q r) -> p n q r", r=R),
+                                 in_=accs[(i, K, h)].rearrange("p (r n q) -> p n q r", r=R, n=2),
+                                 func=ACT.Relu, bias=bias[:, K - 2, i:i + 1])
+
+        def maxi(i, K, lay):
+            n0, nt = lay
+            v = T + 1 - K
+            nc.vector.tensor_tensor(out=Tn[:, i, n0:n0 + nt, 0:v], in0=Tn[:, i, n0:n0 + nt, 0:v],
+                                    in1=tmps[(i, K, n0, nt)][:, :, 0:v], op=ALU.max)
+
+        def square(i, lay):
+            n0, nt = lay
+            if i == 0:
+                nc.scalar.activation(out=ssum[:], in_=Tn[:, i], func=ACT.Square)
+            else:
+                sq = epool.tile([P, nt, T], F32, name="sq", tag="sq")
+                sqs[(i, n0)] = sq
+                nc.scalar.activation(out=sq[:], in_=Tn[:, i, n0:n0 + nt, :], func=ACT.Square)
+
+        def addsq(i, lay):
+            n0, nt = lay
+            if i > 0:
+                nc.vector.tensor_tensor(out=ssum[:, n0:n0 + nt, :], in0=ssum[:, n0:n0 + nt, :],
+                                        in1=sqs[(i, n0)][:], op=ALU.add)
+
+        def norm_sum(lay, whole):
+            n0, nt = lay
+            rb = tp.tile([P, P * nt], F32, name="rb", tag="tp")
+            rbs[n0] = rb
+            nc.tensor.matmul(out=rb[:], lhsT=ones[:], rhs=ssum[:, n0:n0 + nt, :].rearrange("p n q -> p (n q)"),
+                             start=True, stop=whole)
+
+        def norm_last(lay):
+            n0, nt = lay
+            nc.tensor.matmul(out=rbs[n0][:], lhsT=ones[:], rhs=sqs[(NI - 1, n0)][:].rearrange("p n q -> p (n q)"),
+                             start=False, stop=True)
+
+        def rsqrt(lay):
+            n0, nt = lay
+            nc.scalar.activation(out=rinv[:, n0:n0 + nt, :].rearrange("p n q -> p (n q)"), in_=rbs[n0][:],
+                                 func=ACT.Abs_reciprocal_sqrt)
+
+        def scale_store(n):
+            nc.vector.scalar_tensor_tensor(
+                out=O[:, n, :].rearrange("p (i q) -> p i q", i=NI),
+                in0=rinv[:, n, 0:T - 1].unsqueeze(1).to_broadcast([P, NI, T - 1]),
+                scalar=1e12, in1=Tn[:, :, n, 0:T - 1], op0=ALU.min, op1=ALU.mult)
+            nc.sync.dma_start(out=out[n].rearrange("(m i) q -> m (i q)", i=NI), in_=O[:, n, :])
+
+        def lay_of(i):
+            if paired(i):
+                return FULL
+            return HALF[0]
+
+        def halves_of(i):
+            if paired(i):
+                return (0, 1)
+            return (0,)
+
+        def prod_now(i, K):
+            for h in halves_of(i):
+                products(i, K, h)
+
+        def relu_now(i, K):
+            for h in halves_of(i):
+                relu(i, K, h)
+
+        tx(0, "V")
+        tx(1, "S")
+        quant_h(0, 0, 4)
+        transposes(0, 2, "SS")
+        shift(0)
+        quant_h(0, 4, 2)
+        quantise(0, 2)
+        quant_h(0, 6, 1)
+        tx(2, "V")
+        tx(3, "S")
+        products(0, 2, 0)
+        quant_h(1, 0, 4)
+        shift(1)
+        quant_h(1, 4, 2)
+        quant_h(1, 6, 1)
+        for K in WIDTHS:
+            nc.vector.tensor_copy(out=bias[:, K - 2, :], in_=braw[K][:])
+        transposes(0, 3, "SVS")
+        quantise(0, 3)
+        products(0, 2, 1)
+        relu_now(0, 2)
+        transposes(0, 4, "VSVS")
+        quantise(0, 4)
+        prod_now(0, 3)
+        relu_now(0, 3)
+        maxi(0, 3, FULL)
+        transposes(1, 2, "SS")
+        quantise(1, 2)
+        transposes(1, 3, "SVS")
+        quantise(1, 3)
+        prod_now(0, 4)
+        last = NI - 1
+        prev = 0
+        for a in (1, 3, 5):
+            units = [(a, 4), (a + 1, 2), (a + 1, 3), (a + 1, 4), (a + 2, 2), (a + 2, 3)]
+            tiles = [a, a + 1]
+            if a + 2 == last:
+                units.append((last, 4))
+                tiles.append(last)
+            b = 0
+            for (i, K) in units:
+                transposes(i, K, ALT[b % 2:b % 2 + K])
+                b += K
+            relu_now(prev, 4)
+            quantise(a, 4)
+            maxi(prev, 4, lay_of(prev))
+            todo = units[1:]
+            for idx in range(len(tiles)):
+                i = tiles[idx]
+                prod_now(i, 2)
+                relu_now(i, 2)
+                if 3 * idx < len(todo):
+                    quantise(*todo[3 * idx])
+                square(prev, lay_of(prev))
+                if 3 * idx + 1 < len(todo):
+                    quantise(*todo[3 * idx + 1])
+                addsq(prev, lay_of(prev))
+                prod_now(i, 3)
+                relu_now(i, 3)
+                if 3 * idx + 2 < len(todo):
+                    quantise(*todo[3 * idx + 2])
+                maxi(i, 3, lay_of(i))
+                prod_now(i, 4)
+                if idx < len(tiles) - 1:
+                    relu_now(i, 4)
+                    maxi(i, 4, lay_of(i))
+                prev = i
+        hA = HALF[0]
+        hB = HALF[1]
+        relu(last, 4, 0)
+        products(last, 2, 1)
+        relu(last, 2, 1)
+        maxi(last, 4, hA)
+        square(last, hA)
+        addsq(last, hA)
+        products(last, 3, 1)
+        relu(last, 3, 1)
+        maxi(last, 3, hB)
+        products(last, 4, 1)
+        norm_sum(hA, True)
+        relu(last, 4, 1)
+        rsqrt(hA)
+        maxi(last, 4, hB)
+        norm_sum(hB, False)
+        square(last, hB)
+        norm_last(hB)
+        scale_store(0)
+        rsqrt(hB)
+        scale_store(1)
+        scale_store(2)
+        scale_store(3)

@@ -18,15 +18,12 @@ D = 1024
 F = 1024
 NI = F // P
 WIDTHS = (2, 3, 4)
+ORDER = (4, 3, 2)
 R = 4
 NPL = R + 3
 HC = NPL * 64
 FLOPS = 2 * B * (127 * 2 + 126 * 3 + 125 * 4) * D * F
-MANUAL = True
-LAST = 1
-ALT = "VSVSVSVS"
-FULL = (0, 4)
-HALF = ((0, 2), (2, 2))
+OTHER_BANK = ((0, 2), (NI - 2, 2), (NI - 1, 4), (NI - 1, 3), (NI - 1, 2))
 QCALLS = {2: ((0, 2048),), 3: ((0, 2048), (2048, 1024)), 4: ((0, 4096),)}
 
 
@@ -35,15 +32,23 @@ def tile_textheading_pa_kernel(tc, words_emb, W2, b2, W3, b3, W4, b4, out):
     Wd = {2: W2, 3: W3, 4: W4}
     bd = {2: b2, 3: b3, 4: b4}
     with ExitStack() as ctx:
-        if MANUAL:
-            ctx.enter_context(tc.manual_schedule())
+        ctx.enter_context(tc.manual_schedule())
         const = ctx.enter_context(tc.tile_pool(name="const", bufs=1))
         wpool = ctx.enter_context(tc.tile_pool(name="wraw", bufs=3))
-        gpool = ctx.enter_context(tc.tile_pool(name="grp", bufs=3))
-        cpool = ctx.enter_context(tc.tile_pool(name="codes", bufs=3))
+        ppool = ctx.enter_context(tc.tile_pool(name="perm", bufs=2))
+        gpool = ctx.enter_context(tc.tile_pool(name="grp", bufs=2))
+        cpool = ctx.enter_context(tc.tile_pool(name="codes", bufs=2))
         epool = ctx.enter_context(tc.tile_pool(name="epi", bufs=2))
-        tp = ctx.enter_context(tc.psum_pool(name="tp", bufs=5))
-        accp = ctx.enter_context(tc.psum_pool(name="acc", bufs=1))
+        psum = ctx.enter_context(tc.psum_pool(name="psum", bufs=1))
+        ring = ["b%d" % b for b in range(6)]
+
+        def bank_of(tag):
+            return psum.tile([P, 512], F32, name="bank_" + tag, tag=tag)
+
+        def next_bank():
+            tag = ring.pop(0)
+            ring.append(tag)
+            return bank_of(tag)
 
         ident = const.tile([P, P], F32, name="ident")
         make_identity(nc, ident[:])
@@ -67,8 +72,9 @@ def tile_textheading_pa_kernel(tc, words_emb, W2, b2, W3, b3, W4, b4, out):
             nc.sync.dma_start(out=x_sb[:, n, :], in_=words_emb[n])
 
         def load_w(i, K):
-            wraw[(i, K)] = wpool.tile([P, K * D], BF16, name="w%d" % K, tag="w%d" % K)
-            nc.sync.dma_start(out=wraw[(i, K)][:], in_=Wv[K][i])
+            if i < NI:
+                wraw[(i, K)] = wpool.tile([P, K * D], BF16, name="w%d" % K, tag="w%d" % K)
+                nc.sync.dma_start(out=wraw[(i, K)][:], in_=Wv[K][i])
 
         load_x(0)
         load_x(1)
@@ -78,7 +84,7 @@ def tile_textheading_pa_kernel(tc, words_emb, W2, b2, W3, b3, W4, b4, out):
         load_w(0, 3)
         load_w(0, 4)
         for i in (1, 2):
-            for K in WIDTHS:
+            for K in ORDER:
                 load_w(i, K)
 
         def copy(eng, dst, src):
@@ -100,7 +106,7 @@ def tile_textheading_pa_kernel(tc, words_emb, W2, b2, W3, b3, W4, b4, out):
                 nc.vector.memset(xgw[h][:, g, R:NPL, :, 31:32, :], 0.0)
 
         def tx(n, eng):
-            xb = tp.tile([P, 2, 2, P], F32, name="xb", tag="tp")
+            xb = next_bank()[:].rearrange("p (g u f) -> p g u f", g=2, u=2)
             xw = x_sb[:, n, :].bitcast(F32)
             for g in range(2):
                 for u in range(2):
@@ -120,23 +126,39 @@ def tile_textheading_pa_kernel(tc, words_emb, W2, b2, W3, b3, W4, b4, out):
                 nc.vector.quantize_mx(out=xch[h][:, g, c0:c0 + w].bitcast(FP8X4), scales=xsh[h][:, g, c0:c0 + w],
                                       in_=xgh[h][:, a:a + 4 * w])
 
+        perm = {}
+        turned = {}
         grp = {}
         cod = {}
 
-        def transposes(i, K, engs):
+        def permute(i, K, eng):
+            if i < NI:
+                pt = ppool.tile([P, K * D], BF16, name="p%d" % K, tag="p%d" % K)
+                perm[(i, K)] = pt[:].bitcast(F32).rearrange("p (u w) -> p u w", u=2)
+                copy(eng, perm[(i, K)], wraw[(i, K)][:].bitcast(F32).rearrange("p (w u) -> p u w", u=2))
+                load_w(i + 3, K)
+
+        def transposes(i, K):
+            banks = []
+            for k in range(K):
+                bank = next_bank()[:].rearrange("p (g u f) -> p g u f", g=2, u=2)
+                banks.append(bank)
+                for g in range(2):
+                    for u in range(2):
+                        o = 256 * k + 128 * g
+                        if (i, K) in perm:
+                            words = perm[(i, K)][:, u, o:o + P]
+                        else:
+                            words = wraw[(i, K)][:].bitcast(F32)[:, 2 * o + u:2 * (o + P):2]
+                        nc.tensor.transpose(bank[:, g, u, :], words, ident[:])
+            turned[(i, K)] = banks
+
+        def regroup(i, K, engs):
             gr = gpool.tile([P, K * 1024], BF16, name="g%d" % K, tag="g%d" % K, align_bytes=64)
             grp[(i, K)] = gr
             gr_w = gr[:].bitcast(F32).rearrange("p (k g f u) -> p k g f u", k=K, g=2, f=P, u=2)
-            ww = wraw[(i, K)][:].bitcast(F32)
             for k in range(K):
-                bank = tp.tile([P, 2, 2, P], F32, name="bank", tag="tp")
-                for g in range(2):
-                    for u in range(2):
-                        o = 512 * k + 256 * g
-                        nc.tensor.transpose(bank[:, g, u, :], ww[:, o + u:o + 256:2], ident[:])
-                copy(engs[k], gr_w[:, k], bank[:].rearrange("p g u f -> p g f u"))
-            if i + 3 < NI:
-                load_w(i + 3, K)
+                copy(engs[k], gr_w[:, k], turned[(i, K)][k].rearrange("p g u f -> p g f u"))
 
         def quantise(i, K):
             cw = cpool.tile([P, K * 256], U32, name="c%d" % K, tag="c%d" % K, align_bytes=64)
@@ -147,122 +169,103 @@ def tile_textheading_pa_kernel(tc, words_emb, W2, b2, W3, b3, W4, b4, out):
                 nc.vector.quantize_mx(out=cw[:, a // 4:(a + w) // 4].bitcast(FP8X4),
                                       scales=sc[:, a // 4:(a + w) // 4], in_=gr[:, a:a + w])
 
-        Tn = const.tile([P, NI, B, T], F32, name="Tn")
-        ssum = const.tile([P, B, T], F32, name="ssum")
-        rinv = const.tile([P, B, T], F32, name="rinv")
+        Tn = const.tile([P, NI, B * T], F32, name="Tn")
+        ssum = const.tile([P, B * T], F32, name="ssum")
+        rinv = const.tile([P, B * T], F32, name="rinv")
         O = const.tile([P, B, NI * (T - 1)], F32, name="O")
         accs = {}
-        tmps = {}
+        acc_tags = {}
+        sums = ["s0", "s1"]
+        for i in range(NI):
+            for K in (ORDER if i > 0 else WIDTHS):
+                if (i, K) not in OTHER_BANK:
+                    acc_tags[(i, K)] = sums[0]
+                    sums.reverse()
         sqs = {}
         rbs = {}
 
-        def paired(i):
-            return i < NI - LAST
-
         def products(i, K, h):
-            if paired(i):
-                if h == 0:
-                    acc = accp.tile([P, 512], F32, name="acc%d" % K, tag="acc%d" % K)
-                    accs[(i, K, 0)] = acc[:, 0:256]
-                    accs[(i, K, 1)] = acc[:, 256:512]
-            else:
-                acch = accp.tile([P, 256], F32, name="acc%d" % K, tag="acc%d" % K)
-                accs[(i, K, h)] = acch[:]
+            if h == 0:
+                accs[(i, K)] = bank_of(acc_tags[(i, K)]) if (i, K) in acc_tags else next_bank()
             cw, sc = cod[(i, K)]
             for k in range(K):
                 for g in range(2):
                     j = (2 * k + g) * P
-                    nc.tensor.matmul_mx(out=accs[(i, K, h)], lhsT=cw[:, j:j + P].bitcast(FP8X4),
-                                        lhsT_scale=sc[:, j:j + P],
+                    nc.tensor.matmul_mx(out=accs[(i, K)][:, 256 * h:256 * h + 256],
+                                        lhsT=cw[:, j:j + P].bitcast(FP8X4), lhsT_scale=sc[:, j:j + P],
                                         rhs=xch[h][:, g, 64 * k:64 * k + 256].bitcast(FP8X4),
                                         rhs_scale=xsh[h][:, g, 64 * k:64 * k + 256],
                                         start=(k == 0 and g == 0), stop=(k == K - 1 and g == 1))
 
-        def relu(i, K, h):
-            if K == 2:
-                dst = Tn[:, i, 2 * h:2 * h + 2, :]
-            elif paired(i):
-                if h == 0:
-                    tf = epool.tile([P, B, T], F32, name="t%d" % K, tag="t%d" % K)
-                    tmps[(i, K, 0, 4)] = tf[:]
-                    tmps[(i, K, 0, 2)] = tf[:, 0:2, :]
-                    tmps[(i, K, 2, 2)] = tf[:, 2:4, :]
-                dst = tmps[(i, K, 2 * h, 2)]
-            else:
-                th = epool.tile([P, 2, T], F32, name="t%d" % K, tag="t%d" % K)
-                tmps[(i, K, 2 * h, 2)] = th[:]
-                dst = th[:]
-            nc.scalar.activation(out=dst.rearrange("p n (q r) -> p n q r", r=R),
-                                 in_=accs[(i, K, h)].rearrange("p (r n q) -> p n q r", r=R, n=2),
-                                 func=ACT.Relu, bias=bias[:, K - 2, i:i + 1])
+        def relu(dst, i, K, h0, nh):
+            nc.scalar.activation(
+                out=dst.rearrange("p (h m r) -> p h m r", h=nh, r=R),
+                in_=accs[(i, K)][:, 256 * h0:256 * (h0 + nh)].rearrange("p (h r m) -> p h m r", h=nh, r=R),
+                func=ACT.Relu, bias=bias[:, K - 2, i:i + 1])
 
-        def maxi(i, K, lay):
-            n0, nt = lay
-            v = T + 1 - K
-            nc.vector.tensor_tensor(out=Tn[:, i, n0:n0 + nt, 0:v], in0=Tn[:, i, n0:n0 + nt, 0:v],
-                                    in1=tmps[(i, K, n0, nt)][:, :, 0:v], op=ALU.max)
+        def first(i, h0, nh):
+            relu(Tn[:, i, 256 * h0:256 * (h0 + nh)], i, 4, h0, nh)
 
-        def square(i, lay):
-            n0, nt = lay
+        def clear(eng, i, h0, nh, K):
+            eng.memset(Tn[:, i, 256 * h0:256 * (h0 + nh)].rearrange("p (n t) -> p n t", t=T)[:, :, T + 1 - K:T - 1], 0.0)
+
+        def more(i, K, h):
+            dst = Tn[:, i, 256 * h:256 * h + 256].rearrange("p (m r) -> p m r", r=R)
+            nc.vector.scalar_tensor_tensor(
+                out=dst, in0=accs[(i, K)][:, 256 * h:256 * h + 256].rearrange("p (r m) -> p m r", r=R),
+                scalar=bias[:, K - 2, i:i + 1], in1=dst, op0=ALU.add, op1=ALU.max)
+
+        def square(i, h0, nh):
+            c0, c1 = 256 * h0, 256 * (h0 + nh)
             if i == 0:
-                nc.scalar.activation(out=ssum[:], in_=Tn[:, i], func=ACT.Square)
+                nc.scalar.activation(out=ssum[:], in_=Tn[:, 0], func=ACT.Square)
             else:
-                sq = epool.tile([P, nt, T], F32, name="sq", tag="sq")
-                sqs[(i, n0)] = sq
-                nc.scalar.activation(out=sq[:], in_=Tn[:, i, n0:n0 + nt, :], func=ACT.Square)
+                sq = epool.tile([P, c1 - c0], F32, name="sq", tag="sq")
+                sqs[(i, h0)] = sq
+                nc.scalar.activation(out=sq[:], in_=Tn[:, i, c0:c1], func=ACT.Square)
 
-        def addsq(i, lay):
-            n0, nt = lay
+        def square_v(i, h):
+            sq = epool.tile([P, 256], F32, name="sq", tag="sq")
+            sqs[(i, h)] = sq
+            t = Tn[:, i, 256 * h:256 * h + 256]
+            nc.vector.tensor_tensor(out=sq[:], in0=t, in1=t, op=ALU.mult)
+
+        def addsq(i, h0, nh):
+            c0, c1 = 256 * h0, 256 * (h0 + nh)
             if i > 0:
-                nc.vector.tensor_tensor(out=ssum[:, n0:n0 + nt, :], in0=ssum[:, n0:n0 + nt, :],
-                                        in1=sqs[(i, n0)][:], op=ALU.add)
+                nc.vector.tensor_tensor(out=ssum[:, c0:c1], in0=ssum[:, c0:c1], in1=sqs[(i, h0)][:], op=ALU.add)
 
-        def norm_sum(lay, whole):
-            n0, nt = lay
-            rb = tp.tile([P, P * nt], F32, name="rb", tag="tp")
-            rbs[n0] = rb
-            nc.tensor.matmul(out=rb[:], lhsT=ones[:], rhs=ssum[:, n0:n0 + nt, :].rearrange("p n q -> p (n q)"),
-                             start=True, stop=whole)
+        def norm(h, src, start, stop):
+            if start:
+                rbs[h] = next_bank()
+            nc.tensor.matmul(out=rbs[h][:, 0:256], lhsT=ones[:], rhs=src, start=start, stop=stop)
 
-        def norm_last(lay):
-            n0, nt = lay
-            nc.tensor.matmul(out=rbs[n0][:], lhsT=ones[:], rhs=sqs[(NI - 1, n0)][:].rearrange("p n q -> p (n q)"),
-                             start=False, stop=True)
+        def rsqrt(h):
+            nc.scalar.activation(out=rinv[:, 256 * h:256 * h + 256], in_=rbs[h][:, 0:256], func=ACT.Abs_reciprocal_sqrt)
 
-        def rsqrt(lay):
-            n0, nt = lay
-            nc.scalar.activation(out=rinv[:, n0:n0 + nt, :].rearrange("p n q -> p (n q)"), in_=rbs[n0][:],
-                                 func=ACT.Abs_reciprocal_sqrt)
+        def scale(n, i0, i1):
+            nc.vector.scalar_tensor_tensor(
+                out=O[:, n, :].rearrange("p (i q) -> p i q", i=NI)[:, i0:i1, :],
+                in0=rinv[:, T * n:T * n + T - 1].unsqueeze(1).to_broadcast([P, i1 - i0, T - 1]),
+                scalar=1e12, in1=Tn[:, i0:i1, T * n:T * n + T - 1], op0=ALU.min, op1=ALU.mult)
+
+        def store(n, c0, c1):
+            nc.sync.dma_start(out=out[n].rearrange("(m i) q -> m (i q)", i=NI)[:, c0:c1], in_=O[:, n, c0:c1])
 
         def scale_store(n):
-            nc.vector.scalar_tensor_tensor(
-                out=O[:, n, :].rearrange("p (i q) -> p i q", i=NI),
-                in0=rinv[:, n, 0:T - 1].unsqueeze(1).to_broadcast([P, NI, T - 1]),
-                scalar=1e12, in1=Tn[:, :, n, 0:T - 1], op0=ALU.min, op1=ALU.mult)
-            nc.sync.dma_start(out=out[n].rearrange("(m i) q -> m (i q)", i=NI), in_=O[:, n, :])
+            scale(n, 0, NI)
+            store(n, 0, NI * (T - 1))
 
-        def lay_of(i):
-            if paired(i):
-                return FULL
-            return HALF[0]
-
-        def halves_of(i):
-            if paired(i):
-                return (0, 1)
-            return (0,)
-
-        def prod_now(i, K):
-            for h in halves_of(i):
-                products(i, K, h)
-
-        def relu_now(i, K):
-            for h in halves_of(i):
-                relu(i, K, h)
+        def both(f, i, K):
+            f(i, K, 0)
+            f(i, K, 1)
 
         tx(0, "V")
         tx(1, "S")
         quant_h(0, 0, 4)
-        transposes(0, 2, "SS")
+        transposes(0, 2)
+        regroup(0, 2, "SS")
+        load_w(3, 2)
         shift(0)
         quant_h(0, 4, 2)
         quantise(0, 2)
@@ -276,77 +279,120 @@ def tile_textheading_pa_kernel(tc, words_emb, W2, b2, W3, b3, W4, b4, out):
         quant_h(1, 6, 1)
         for K in WIDTHS:
             nc.vector.tensor_copy(out=bias[:, K - 2, :], in_=braw[K][:])
-        transposes(0, 3, "SVS")
-        quantise(0, 3)
+        transposes(0, 3)
+        regroup(0, 3, "SSS")
+        load_w(3, 3)
         products(0, 2, 1)
-        relu_now(0, 2)
-        transposes(0, 4, "VSVS")
+        quantise(0, 3)
+        t2 = epool.tile([P, B * T], F32, name="t2", tag="sq")
+        relu(t2[:], 0, 2, 0, 2)
+        transposes(0, 4)
+        regroup(0, 4, "SSSS")
+        load_w(3, 4)
+        permute(1, 4, "V")
+        both(products, 0, 3)
+        permute(1, 3, "V")
         quantise(0, 4)
-        prod_now(0, 3)
-        relu_now(0, 3)
-        maxi(0, 3, FULL)
-        transposes(1, 2, "SS")
-        quantise(1, 2)
-        transposes(1, 3, "SVS")
+        permute(1, 2, "V")
+        transposes(1, 4)
+        regroup(1, 4, "SSSS")
+        permute(2, 4, "V")
+        transposes(1, 3)
+        regroup(1, 3, "SSS")
+        quantise(1, 4)
+        permute(2, 3, "V")
+        transposes(1, 2)
+        regroup(1, 2, "SS")
+        permute(2, 2, "V")
+        both(products, 0, 4)
+        first(0, 0, 2)
+        clear(nc.gpsimd, 0, 0, 2, 4)
         quantise(1, 3)
-        prod_now(0, 4)
-        last = NI - 1
-        prev = 0
-        for a in (1, 3, 5):
-            units = [(a, 4), (a + 1, 2), (a + 1, 3), (a + 1, 4), (a + 2, 2), (a + 2, 3)]
-            tiles = [a, a + 1]
-            if a + 2 == last:
-                units.append((last, 4))
-                tiles.append(last)
-            b = 0
-            for (i, K) in units:
-                transposes(i, K, ALT[b % 2:b % 2 + K])
-                b += K
-            relu_now(prev, 4)
-            quantise(a, 4)
-            maxi(prev, 4, lay_of(prev))
-            todo = units[1:]
-            for idx in range(len(tiles)):
-                i = tiles[idx]
-                prod_now(i, 2)
-                relu_now(i, 2)
-                if 3 * idx < len(todo):
-                    quantise(*todo[3 * idx])
-                square(prev, lay_of(prev))
-                if 3 * idx + 1 < len(todo):
-                    quantise(*todo[3 * idx + 1])
-                addsq(prev, lay_of(prev))
-                prod_now(i, 3)
-                relu_now(i, 3)
-                if 3 * idx + 2 < len(todo):
-                    quantise(*todo[3 * idx + 2])
-                maxi(i, 3, lay_of(i))
-                prod_now(i, 4)
-                if idx < len(tiles) - 1:
-                    relu_now(i, 4)
-                    maxi(i, 4, lay_of(i))
-                prev = i
-        hA = HALF[0]
-        hB = HALF[1]
-        relu(last, 4, 0)
-        products(last, 2, 1)
-        relu(last, 2, 1)
-        maxi(last, 4, hA)
-        square(last, hA)
-        addsq(last, hA)
-        products(last, 3, 1)
-        relu(last, 3, 1)
-        maxi(last, 3, hB)
-        products(last, 4, 1)
-        norm_sum(hA, True)
-        relu(last, 4, 1)
-        rsqrt(hA)
-        maxi(last, 4, hB)
-        norm_sum(hB, False)
-        square(last, hB)
-        norm_last(hB)
+        both(more, 0, 3)
+        clear(nc.gpsimd, 0, 0, 2, 3)
+        quantise(1, 2)
+        for s in range(1, NI - 1):
+            j = s + 1
+            transposes(j, 4)
+            regroup(j, 4, "SSSS")
+            if s > 1:
+                clear(nc.gpsimd, s - 1, 0, 2, 4)
+                both(more, s - 1, 3)
+                clear(nc.gpsimd, s - 1, 0, 2, 3)
+                permute(s + 1, 2, "V")
+                both(more, s - 1, 2)
+            else:
+                nc.vector.tensor_tensor(out=Tn[:, 0], in0=Tn[:, 0], in1=t2[:], op=ALU.max)
+            transposes(j, 3)
+            regroup(j, 3, "SSS")
+            quantise(j, 4)
+            permute(s + 2, 4, "V")
+            quantise(j, 3)
+            transposes(j, 2)
+            permute(s + 2, 3, "V")
+            if s < NI - 2:
+                regroup(j, 2, "SS")
+                quantise(j, 2)
+                both(products, s, 4)
+                first(s, 0, 2)
+                square(s - 1, 0, 2)
+                addsq(s - 1, 0, 2)
+                both(products, s, 3)
+                both(products, s, 2)
+        a = NI - 2
+        b = NI - 1
+        products(a, 4, 0)
+        first(a, 0, 1)
+        regroup(b, 2, "SS")
+        square(a - 1, 0, 2)
+        products(a, 3, 0)
+        clear(nc.vector, a, 0, 1, 4)
+        more(a, 3, 0)
+        clear(nc.vector, a, 0, 1, 3)
+        quantise(b, 2)
+        addsq(a - 1, 0, 2)
+        products(a, 2, 0)
+        more(a, 2, 0)
+        products(b, 4, 0)
+        first(b, 0, 1)
+        square(a, 0, 1)
+        clear(nc.vector, b, 0, 1, 4)
+        products(b, 3, 0)
+        more(b, 3, 0)
+        addsq(a, 0, 1)
+        clear(nc.vector, b, 0, 1, 3)
+        products(b, 2, 0)
+        more(b, 2, 0)
+        square_v(b, 0)
+        products(a, 4, 1)
+        first(a, 1, 1)
+        addsq(b, 0, 1)
+        products(a, 3, 1)
+        clear(nc.vector, a, 1, 1, 4)
+        more(a, 3, 1)
+        clear(nc.vector, a, 1, 1, 3)
+        products(a, 2, 1)
+        norm(0, ssum[:, 0:256], True, True)
+        rsqrt(0)
+        more(a, 2, 1)
+        square(a, 1, 1)
+        products(b, 4, 1)
+        first(b, 1, 1)
         scale_store(0)
-        rsqrt(hB)
+        addsq(a, 1, 1)
+        clear(nc.vector, b, 1, 1, 4)
+        products(b, 3, 1)
+        more(b, 3, 1)
+        clear(nc.vector, b, 1, 1, 3)
+        products(b, 2, 1)
+        norm(1, ssum[:, 256:512], True, False)
+        more(b, 2, 1)
+        square_v(b, 1)
+        norm(1, sqs[(b, 1)][:], False, True)
         scale_store(1)
+        rsqrt(1)
         scale_store(2)
-        scale_store(3)
+        scale(3, 0, 5)
+        store(3, 0, 608)
+        scale(3, 5, NI)
+        store(3, 608, NI * (T - 1))

@@ -319,7 +319,6 @@ def tile_textheading_pa_kernel(tc, words_emb, W2, b2, W3, b3, W4, b4, out):
                 clear(nc.gpsimd, s - 1, 0, 2, 4)
                 both(more, s - 1, 3)
                 clear(nc.gpsimd, s - 1, 0, 2, 3)
-                permute(s + 1, 2, "V")
                 both(more, s - 1, 2)
             else:
                 nc.vector.tensor_tensor(out=Tn[:, 0], in0=Tn[:, 0], in1=t2[:], op=ALU.max)
@@ -336,6 +335,7 @@ def tile_textheading_pa_kernel(tc, words_emb, W2, b2, W3, b3, W4, b4, out):
                 both(products, s, 4)
                 first(s, 0, 2)
                 square(s - 1, 0, 2)
+                permute(s + 2, 2, "S")
                 addsq(s - 1, 0, 2)
                 both(products, s, 3)
                 both(products, s, 2)

@@ -6,6 +6,7 @@ from concourse.masks import make_identity
 F32 = mybir.dt.float32
 BF16 = mybir.dt.bfloat16
 U32 = mybir.dt.uint32
+I32 = mybir.dt.int32
 U8 = mybir.dt.uint8
 FP8X4 = mybir.dt.float8_e4m3fn_x4
 ACT = mybir.ActivationFunctionType
@@ -21,9 +22,9 @@ WIDTHS = (2, 3, 4)
 ORDER = (4, 3, 2)
 R = 4
 NPL = R + 3
-HC = NPL * 64
+HC = NPL * P
 FLOPS = 2 * B * (127 * 2 + 126 * 3 + 125 * 4) * D * F
-OTHER_BANK = ((0, 2), (NI - 2, 2), (NI - 1, 4), (NI - 1, 3), (NI - 1, 2))
+OTHER_BANK = ((NI - 2, 2), (NI - 1, 4), (NI - 1, 3), (NI - 1, 2))
 QCALLS = {2: ((0, 2048),), 3: ((0, 2048), (2048, 1024)), 4: ((0, 4096),)}
 
 
@@ -76,13 +77,10 @@ def tile_textheading_pa_kernel(tc, words_emb, W2, b2, W3, b3, W4, b4, out):
                 wraw[(i, K)] = wpool.tile([P, K * D], BF16, name="w%d" % K, tag="w%d" % K)
                 nc.sync.dma_start(out=wraw[(i, K)][:], in_=Wv[K][i])
 
-        load_x(0)
-        load_x(1)
-        load_w(0, 2)
-        load_x(2)
-        load_x(3)
-        load_w(0, 3)
-        load_w(0, 4)
+        for n in range(B):
+            load_x(n)
+        for K in WIDTHS:
+            load_w(0, K)
         for i in (1, 2):
             for K in ORDER:
                 load_w(i, K)
@@ -93,17 +91,17 @@ def tile_textheading_pa_kernel(tc, words_emb, W2, b2, W3, b3, W4, b4, out):
             else:
                 nc.scalar.copy(out=dst, in_=src)
 
-        xgh = []
-        xgw = []
+        xg = const.tile([P, 2 * HC * 4], BF16, name="xg", align_bytes=64)
+        xgw = xg[:].bitcast(F32).rearrange("p (g r n q u) -> p g r n q u", g=2, r=NPL, n=B, q=32, u=2)
+        xc = const.tile([P, 2, HC], U32, name="xc", align_bytes=64)
+        xs = const.tile([P, 2, HC], U8, name="xs", align_bytes=64)
+        for g in range(2):
+            nc.vector.memset(xgw[:, g, R:NPL, :, 31:32, :], 0.0)
         xch = []
         xsh = []
         for h in range(2):
-            xgh.append(const.tile([P, 2 * HC * 4], BF16, name="xgh%d" % h, align_bytes=64))
-            xgw.append(xgh[h][:].bitcast(F32).rearrange("p (g r n q u) -> p g r n q u", g=2, r=NPL, n=2, q=32, u=2))
-            xch.append(const.tile([P, 2, HC], U32, name="xch%d" % h, align_bytes=64))
-            xsh.append(const.tile([P, 2, HC], U8, name="xsh%d" % h, align_bytes=64))
-            for g in range(2):
-                nc.vector.memset(xgw[h][:, g, R:NPL, :, 31:32, :], 0.0)
+            xch.append(const.tile([P, 2, NPL * 64], U32, name="xch%d" % h, align_bytes=64))
+            xsh.append(const.tile([P, 2, NPL * 64], U8, name="xsh%d" % h, align_bytes=64))
 
         def tx(n, eng):
             xb = next_bank()[:].rearrange("p (g u f) -> p g u f", g=2, u=2)
@@ -112,19 +110,27 @@ def tile_textheading_pa_kernel(tc, words_emb, W2, b2, W3, b3, W4, b4, out):
                 for u in range(2):
                     nc.tensor.transpose(xb[:, g, u, :], xw[:, 256 * g + u:256 * (g + 1):2], ident[:])
             for g in range(2):
-                copy(eng, xgw[n // 2][:, g, 0:R, n % 2, :, :], xb[:, g, :, :].rearrange("p u (q r) -> p r q u", r=R))
+                copy(eng, xgw[:, g, 0:R, n, :, :], xb[:, g, :, :].rearrange("p u (q r) -> p r q u", r=R))
 
-        def shift(h):
+        def shift():
             for g in range(2):
-                nc.vector.tensor_copy(out=xgw[h][:, g, R:NPL, :, 0:31, :], in_=xgw[h][:, g, 0:3, :, 1:32, :])
+                nc.vector.tensor_copy(out=xgw[:, g, R:NPL, :, 0:31, :], in_=xgw[:, g, 0:3, :, 1:32, :])
 
-        def quant_h(h, pl0, npl):
-            c0 = pl0 * 64
-            w = npl * 64
+        def quant_x(pl0, npl):
+            c0 = pl0 * P
+            w = npl * P
             for g in range(2):
                 a = (g * HC + c0) * 4
-                nc.vector.quantize_mx(out=xch[h][:, g, c0:c0 + w].bitcast(FP8X4), scales=xsh[h][:, g, c0:c0 + w],
-                                      in_=xgh[h][:, a:a + 4 * w])
+                nc.vector.quantize_mx(out=xc[:, g, c0:c0 + w].bitcast(FP8X4), scales=xs[:, g, c0:c0 + w],
+                                      in_=xg[:, a:a + 4 * w])
+
+        def halve(h):
+            nc.vector.tensor_copy(
+                out=xch[h][:].bitcast(I32).rearrange("p g (r m) -> p (g r) m", r=NPL),
+                in_=xc[:].bitcast(I32).rearrange("p g (r m) -> p (g r) m", r=NPL)[:, :, 64 * h:64 * h + 64])
+            nc.vector.tensor_copy(
+                out=xsh[h][:].rearrange("p g (r m) -> p (g r) m", r=NPL),
+                in_=xs[:].rearrange("p g (r m) -> p (g r) m", r=NPL)[:, :, 64 * h:64 * h + 64])
 
         perm = {}
         turned = {}
@@ -185,44 +191,48 @@ def tile_textheading_pa_kernel(tc, words_emb, W2, b2, W3, b3, W4, b4, out):
         rbs = {}
 
         def products(i, K, h):
-            if h == 0:
+            if h != 1:
                 accs[(i, K)] = bank_of(acc_tags[(i, K)]) if (i, K) in acc_tags else next_bank()
             cw, sc = cod[(i, K)]
+            if h is None:
+                c, s, m, o = xc, xs, P, accs[(i, K)][:]
+            else:
+                c, s, m, o = xch[h], xsh[h], 64, accs[(i, K)][:, 256 * h:256 * h + 256]
             for k in range(K):
                 for g in range(2):
                     j = (2 * k + g) * P
-                    nc.tensor.matmul_mx(out=accs[(i, K)][:, 256 * h:256 * h + 256],
-                                        lhsT=cw[:, j:j + P].bitcast(FP8X4), lhsT_scale=sc[:, j:j + P],
-                                        rhs=xch[h][:, g, 64 * k:64 * k + 256].bitcast(FP8X4),
-                                        rhs_scale=xsh[h][:, g, 64 * k:64 * k + 256],
+                    nc.tensor.matmul_mx(out=o, lhsT=cw[:, j:j + P].bitcast(FP8X4), lhsT_scale=sc[:, j:j + P],
+                                        rhs=c[:, g, m * k:m * k + 4 * m].bitcast(FP8X4),
+                                        rhs_scale=s[:, g, m * k:m * k + 4 * m],
                                         start=(k == 0 and g == 0), stop=(k == K - 1 and g == 1))
 
-        def relu(dst, i, K, h0, nh):
-            nc.scalar.activation(
-                out=dst.rearrange("p (h m r) -> p h m r", h=nh, r=R),
-                in_=accs[(i, K)][:, 256 * h0:256 * (h0 + nh)].rearrange("p (h r m) -> p h m r", h=nh, r=R),
-                func=ACT.Relu, bias=bias[:, K - 2, i:i + 1])
+        def part(ap, h):
+            return ap if h is None else ap[:, 256 * h:256 * h + 256]
 
-        def first(i, h0, nh):
-            relu(Tn[:, i, 256 * h0:256 * (h0 + nh)], i, 4, h0, nh)
+        def relu(dst, i, K, h):
+            nc.scalar.activation(out=dst.rearrange("p (m r) -> p m r", r=R),
+                                 in_=part(accs[(i, K)][:], h).rearrange("p (r m) -> p m r", r=R),
+                                 func=ACT.Relu, bias=bias[:, K - 2, i:i + 1])
 
-        def clear(eng, i, h0, nh, K):
-            eng.memset(Tn[:, i, 256 * h0:256 * (h0 + nh)].rearrange("p (n t) -> p n t", t=T)[:, :, T + 1 - K:T - 1], 0.0)
+        def first(i, h):
+            relu(part(Tn[:, i], h), i, 4, h)
+
+        def clear(eng, i, h, K):
+            eng.memset(part(Tn[:, i], h).rearrange("p (n t) -> p n t", t=T)[:, :, T + 1 - K:T - 1], 0.0)
 
         def more(i, K, h):
-            dst = Tn[:, i, 256 * h:256 * h + 256].rearrange("p (m r) -> p m r", r=R)
+            dst = part(Tn[:, i], h).rearrange("p (m r) -> p m r", r=R)
             nc.vector.scalar_tensor_tensor(
-                out=dst, in0=accs[(i, K)][:, 256 * h:256 * h + 256].rearrange("p (r m) -> p m r", r=R),
+                out=dst, in0=part(accs[(i, K)][:], h).rearrange("p (r m) -> p m r", r=R),
                 scalar=bias[:, K - 2, i:i + 1], in1=dst, op0=ALU.add, op1=ALU.max)
 
-        def square(i, h0, nh):
-            c0, c1 = 256 * h0, 256 * (h0 + nh)
+        def square(i, h):
             if i == 0:
                 nc.scalar.activation(out=ssum[:], in_=Tn[:, 0], func=ACT.Square)
             else:
-                sq = epool.tile([P, c1 - c0], F32, name="sq", tag="sq")
-                sqs[(i, h0)] = sq
-                nc.scalar.activation(out=sq[:], in_=Tn[:, i, c0:c1], func=ACT.Square)
+                sq = epool.tile([P, B * T if h is None else 256], F32, name="sq", tag="sq")
+                sqs[(i, h)] = sq
+                nc.scalar.activation(out=sq[:], in_=part(Tn[:, i], h), func=ACT.Square)
 
         def square_v(i, h):
             sq = epool.tile([P, 256], F32, name="sq", tag="sq")
@@ -230,10 +240,9 @@ def tile_textheading_pa_kernel(tc, words_emb, W2, b2, W3, b3, W4, b4, out):
             t = Tn[:, i, 256 * h:256 * h + 256]
             nc.vector.tensor_tensor(out=sq[:], in0=t, in1=t, op=ALU.mult)
 
-        def addsq(i, h0, nh):
-            c0, c1 = 256 * h0, 256 * (h0 + nh)
+        def addsq(i, h):
             if i > 0:
-                nc.vector.tensor_tensor(out=ssum[:, c0:c1], in0=ssum[:, c0:c1], in1=sqs[(i, h0)][:], op=ALU.add)
+                nc.vector.tensor_tensor(out=part(ssum[:], h), in0=part(ssum[:], h), in1=sqs[(i, h)][:], op=ALU.add)
 
         def norm(h, src, start, stop):
             if start:
@@ -256,46 +265,46 @@ def tile_textheading_pa_kernel(tc, words_emb, W2, b2, W3, b3, W4, b4, out):
             scale(n, 0, NI)
             store(n, 0, NI * (T - 1))
 
-        def both(f, i, K):
-            f(i, K, 0)
-            f(i, K, 1)
+        def busy(n):
+            bank = next_bank()
+            for r in range(n):
+                nc.tensor.matmul(out=bank[:, 0:P], lhsT=ones[:], rhs=ones[:], start=True, stop=True)
 
+        busy(5)
         tx(0, "V")
         tx(1, "S")
-        quant_h(0, 0, 4)
-        transposes(0, 2)
-        regroup(0, 2, "SS")
-        load_w(3, 2)
-        shift(0)
-        quant_h(0, 4, 2)
-        quantise(0, 2)
-        quant_h(0, 6, 1)
         tx(2, "V")
         tx(3, "S")
-        products(0, 2, 0)
-        quant_h(1, 0, 4)
-        shift(1)
-        quant_h(1, 4, 2)
-        quant_h(1, 6, 1)
-        for K in WIDTHS:
-            nc.vector.tensor_copy(out=bias[:, K - 2, :], in_=braw[K][:])
+        busy(1)
+        quant_x(0, 4)
+        transposes(0, 2)
+        regroup(0, 2, "SS")
+        busy(1)
+        shift()
+        quant_x(4, 2)
+        quantise(0, 2)
+        quant_x(6, 1)
         transposes(0, 3)
         regroup(0, 3, "SSS")
-        load_w(3, 3)
-        products(0, 2, 1)
+        busy(2)
+        products(0, 2, None)
+        permute(0, 4, "V")
         quantise(0, 3)
-        t2 = epool.tile([P, B * T], F32, name="t2", tag="sq")
-        relu(t2[:], 0, 2, 0, 2)
+        for K in WIDTHS:
+            nc.vector.tensor_copy(out=bias[:, K - 2, :], in_=braw[K][:])
         transposes(0, 4)
+        t2 = epool.tile([P, B * T], F32, name="t2", tag="sq")
         regroup(0, 4, "SSSS")
-        load_w(3, 4)
+        relu(t2[:], 0, 2, None)
+        load_w(3, 3)
+        load_w(3, 2)
         permute(1, 4, "V")
-        both(products, 0, 3)
+        products(0, 3, None)
         permute(1, 3, "V")
         quantise(0, 4)
         permute(1, 2, "V")
         transposes(1, 4)
-        regroup(1, 4, "SSSS")
+        regroup(1, 4, "SSSV")
         permute(2, 4, "V")
         transposes(1, 3)
         regroup(1, 3, "SSS")
@@ -304,22 +313,22 @@ def tile_textheading_pa_kernel(tc, words_emb, W2, b2, W3, b3, W4, b4, out):
         transposes(1, 2)
         regroup(1, 2, "SS")
         permute(2, 2, "V")
-        both(products, 0, 4)
-        first(0, 0, 2)
-        clear(nc.gpsimd, 0, 0, 2, 4)
+        products(0, 4, None)
+        first(0, None)
+        clear(nc.gpsimd, 0, None, 4)
         quantise(1, 3)
-        both(more, 0, 3)
-        clear(nc.gpsimd, 0, 0, 2, 3)
+        more(0, 3, None)
+        clear(nc.gpsimd, 0, None, 3)
         quantise(1, 2)
         for s in range(1, NI - 1):
             j = s + 1
             transposes(j, 4)
             regroup(j, 4, "SSSS")
             if s > 1:
-                clear(nc.gpsimd, s - 1, 0, 2, 4)
-                both(more, s - 1, 3)
-                clear(nc.gpsimd, s - 1, 0, 2, 3)
-                both(more, s - 1, 2)
+                clear(nc.gpsimd, s - 1, None, 4)
+                more(s - 1, 3, None)
+                clear(nc.gpsimd, s - 1, None, 3)
+                more(s - 1, 2, None)
             else:
                 nc.vector.tensor_tensor(out=Tn[:, 0], in0=Tn[:, 0], in1=t2[:], op=ALU.max)
             transposes(j, 3)
@@ -332,58 +341,60 @@ def tile_textheading_pa_kernel(tc, words_emb, W2, b2, W3, b3, W4, b4, out):
             if s < NI - 2:
                 regroup(j, 2, "SS")
                 quantise(j, 2)
-                both(products, s, 4)
-                first(s, 0, 2)
-                square(s - 1, 0, 2)
+                products(s, 4, None)
+                first(s, None)
+                square(s - 1, None)
                 permute(s + 2, 2, "S")
-                addsq(s - 1, 0, 2)
-                both(products, s, 3)
-                both(products, s, 2)
+                addsq(s - 1, None)
+                products(s, 3, None)
+                products(s, 2, None)
+                if s in (2, 4):
+                    halve(s // 2 - 1)
         a = NI - 2
         b = NI - 1
         products(a, 4, 0)
-        first(a, 0, 1)
+        first(a, 0)
         regroup(b, 2, "SS")
-        square(a - 1, 0, 2)
+        square(a - 1, None)
         products(a, 3, 0)
-        clear(nc.vector, a, 0, 1, 4)
+        clear(nc.vector, a, 0, 4)
         more(a, 3, 0)
-        clear(nc.vector, a, 0, 1, 3)
+        clear(nc.vector, a, 0, 3)
         quantise(b, 2)
-        addsq(a - 1, 0, 2)
+        addsq(a - 1, None)
         products(a, 2, 0)
         more(a, 2, 0)
         products(b, 4, 0)
-        first(b, 0, 1)
-        square(a, 0, 1)
-        clear(nc.vector, b, 0, 1, 4)
+        first(b, 0)
+        square(a, 0)
+        clear(nc.vector, b, 0, 4)
         products(b, 3, 0)
         more(b, 3, 0)
-        addsq(a, 0, 1)
-        clear(nc.vector, b, 0, 1, 3)
+        addsq(a, 0)
+        clear(nc.vector, b, 0, 3)
         products(b, 2, 0)
         more(b, 2, 0)
         square_v(b, 0)
         products(a, 4, 1)
-        first(a, 1, 1)
-        addsq(b, 0, 1)
+        first(a, 1)
+        addsq(b, 0)
         products(a, 3, 1)
-        clear(nc.vector, a, 1, 1, 4)
+        clear(nc.vector, a, 1, 4)
         more(a, 3, 1)
-        clear(nc.vector, a, 1, 1, 3)
+        clear(nc.vector, a, 1, 3)
         products(a, 2, 1)
         norm(0, ssum[:, 0:256], True, True)
         rsqrt(0)
         more(a, 2, 1)
-        square(a, 1, 1)
+        square(a, 1)
         products(b, 4, 1)
-        first(b, 1, 1)
+        first(b, 1)
         scale_store(0)
-        addsq(a, 1, 1)
-        clear(nc.vector, b, 1, 1, 4)
+        addsq(a, 1)
+        clear(nc.vector, b, 1, 4)
         products(b, 3, 1)
         more(b, 3, 1)
-        clear(nc.vector, b, 1, 1, 3)
+        clear(nc.vector, b, 1, 3)
         products(b, 2, 1)
         norm(1, ssum[:, 256:512], True, False)
         more(b, 2, 1)
@@ -391,8 +402,8 @@ def tile_textheading_pa_kernel(tc, words_emb, W2, b2, W3, b3, W4, b4, out):
         norm(1, sqs[(b, 1)][:], False, True)
         scale_store(1)
         rsqrt(1)
-        scale_store(2)
-        scale(3, 0, 5)
-        store(3, 0, 608)
-        scale(3, 5, NI)
-        store(3, 608, NI * (T - 1))
+        for n in (2, 3):
+            scale(n, 0, 5)
+            store(n, 0, 608)
+            scale(n, 5, NI)
+            store(n, 608, NI * (T - 1))

@@ -159,12 +159,13 @@ def tile_textheading_pa_kernel(tc, words_emb, W2, b2, W3, b3, W4, b4, out):
                         nc.tensor.transpose(bank[:, g, u, :], words, ident[:])
             turned[(i, K)] = banks
 
-        def regroup(i, K, engs):
-            gr = gpool.tile([P, K * 1024], BF16, name="g%d" % K, tag="g%d" % K, align_bytes=64)
-            grp[(i, K)] = gr
-            gr_w = gr[:].bitcast(F32).rearrange("p (k g f u) -> p k g f u", k=K, g=2, f=P, u=2)
-            for k in range(K):
-                copy(engs[k], gr_w[:, k], turned[(i, K)][k].rearrange("p g u f -> p g f u"))
+        def regroup(i, K, engs, k0=0):
+            if (i, K) not in grp:
+                grp[(i, K)] = gpool.tile([P, K * 1024], BF16, name="g%d" % K, tag="g%d" % K, align_bytes=64)
+            gr_w = grp[(i, K)][:].bitcast(F32).rearrange("p (k g f u) -> p k g f u", k=K, g=2, f=P, u=2)
+            for k in range(k0, k0 + len(engs)):
+                if engs[k - k0] != "-":
+                    copy(engs[k - k0], gr_w[:, k], turned[(i, K)][k].rearrange("p g u f -> p g f u"))
 
         def quantise(i, K):
             cw = cpool.tile([P, K * 256], U32, name="c%d" % K, tag="c%d" % K, align_bytes=64)
@@ -323,18 +324,22 @@ def tile_textheading_pa_kernel(tc, words_emb, W2, b2, W3, b3, W4, b4, out):
         for s in range(1, NI - 1):
             j = s + 1
             transposes(j, 4)
-            regroup(j, 4, "SSSS")
+            regroup(j, 4, "SSSS" if s == 1 else "S-SS")
             if s > 1:
                 clear(nc.gpsimd, s - 1, None, 4)
                 more(s - 1, 3, None)
                 clear(nc.gpsimd, s - 1, None, 3)
+                regroup(j, 4, "V", 1)
+                if s > 2:
+                    permute(s + 2, 4, "V")
                 more(s - 1, 2, None)
             else:
                 nc.vector.tensor_tensor(out=Tn[:, 0], in0=Tn[:, 0], in1=t2[:], op=ALU.max)
             transposes(j, 3)
             regroup(j, 3, "SSS")
             quantise(j, 4)
-            permute(s + 2, 4, "V")
+            if s <= 2:
+                permute(s + 2, 4, "V")
             quantise(j, 3)
             transposes(j, 2)
             permute(s + 2, 3, "V")

from contextlib import ExitStack

import concourse.mybir as mybir
from concourse.masks import make_identity

F32 = mybir.dt.float32
BF16 = mybir.dt.bfloat16
U32 = mybir.dt.uint32
I32 = mybir.dt.int32
U8 = mybir.dt.uint8
FP8X4 = mybir.dt.float8_e4m3fn_x4
ACT = mybir.ActivationFunctionType
ALU = mybir.AluOpType

P = 128
B = 4
T = 128
D = 1024
F = 1024
NI = F // P
WIDTHS = (2, 3, 4)
ORDER = (4, 3, 2)
R = 4
NPL = R + 3
HC = NPL * P
FLOPS = 2 * B * (127 * 2 + 126 * 3 + 125 * 4) * D * F
OTHER_BANK = ((NI - 2, 2), (NI - 1, 4), (NI - 1, 3), (NI - 1, 2))
QCALLS = {2: ((0, 2048),), 3: ((0, 2048), (2048, 1024)), 4: ((0, 4096),)}


def tile_textheading_pa_kernel(tc, words_emb, W2, b2, W3, b3, W4, b4, out):
    nc = tc.nc
    Wd = {2: W2, 3: W3, 4: W4}
    bd = {2: b2, 3: b3, 4: b4}
    with ExitStack() as ctx:
        ctx.enter_context(tc.manual_schedule())
        const = ctx.enter_context(tc.tile_pool(name="const", bufs=1))
        wpool = ctx.enter_context(tc.tile_pool(name="wraw", bufs=3))
        ppool = ctx.enter_context(tc.tile_pool(name="perm", bufs=2))
        gpool = ctx.enter_context(tc.tile_pool(name="grp", bufs=2))
        cpool = ctx.enter_context(tc.tile_pool(name="codes", bufs=2))
        epool = ctx.enter_context(tc.tile_pool(name="epi", bufs=2))
        psum = ctx.enter_context(tc.psum_pool(name="psum", bufs=1))
        ring = ["b%d" % b for b in range(6)]

        def bank_of(tag):
            return psum.tile([P, 512], F32, name="bank_" + tag, tag=tag)

        def next_bank():
            tag = ring.pop(0)
            ring.append(tag)
            return bank_of(tag)

        ident = const.tile([P, P], F32, name="ident")
        make_identity(nc, ident[:])
        ones = const.tile([P, P], F32, name="ones")
        nc.vector.memset(ones[:], 1.0)
        braw = {}
        for K in WIDTHS:
            braw[K] = const.tile([P, NI], BF16, name="braw%d" % K)
            nc.scalar.dma_start(out=braw[K][:], in_=bd[K].rearrange("(m i) -> m i", i=NI))
        bias = const.tile([P, 3, NI], F32, name="bias")
        warm = const.tile([P, 1], F32, name="warm")
        nc.scalar.activation(out=warm[:], in_=ones[:, 0:1], func=ACT.Abs_reciprocal_sqrt)

        x_sb = const.tile([P, B, D], BF16, name="x_sb")
        Wv = {}
        for K in WIDTHS:
            Wv[K] = Wd[K].rearrange("(m i) k d -> i m (k d)", i=NI)
        wraw = {}

        def load_x(n):
            nc.sync.dma_start(out=x_sb[:, n, :], in_=words_emb[n])

        def load_w(i, K):
            if i < NI:
                wraw[(i, K)] = wpool.tile([P, K * D], BF16, name="w%d" % K, tag="w%d" % K)
                nc.sync.dma_start(out=wraw[(i, K)][:], in_=Wv[K][i])

        for n in range(B):
            load_x(n)
        for K in WIDTHS:
            load_w(0, K)
        for i in (1, 2):
            for K in ORDER:
                load_w(i, K)

        def copy(eng, dst, src):
            if eng == "V":
                nc.vector.tensor_copy(out=dst, in_=src)
            else:
                nc.scalar.copy(out=dst, in_=src)

        xg = const.tile([P, 2 * HC * 4], BF16, name="xg", align_bytes=64)
        xgw = xg[:].bitcast(F32).rearrange("p (g r n q u) -> p g r n q u", g=2, r=NPL, n=B, q=32, u=2)
        xc = const.tile([P, 2, HC], U32, name="xc", align_bytes=64)
        xs = const.tile([P, 2, HC], U8, name="xs", align_bytes=64)
        for g in range(2):
            nc.vector.memset(xgw[:, g, R:NPL, :, 31:32, :], 0.0)
        xch = []
        xsh = []
        for h in range(2):
            xch.append(const.tile([P, 2, NPL * 64], U32, name="xch%d" % h, align_bytes=64))
            xsh.append(const.tile([P, 2, NPL * 64], U8, name="xsh%d" % h, align_bytes=64))

        def tx(n, eng):
            xb = next_bank()[:].rearrange("p (g u f) -> p g u f", g=2, u=2)
            xw = x_sb[:, n, :].bitcast(F32)
            for g in range(2):
                for u in range(2):
                    nc.tensor.transpose(xb[:, g, u, :], xw[:, 256 * g + u:256 * (g + 1):2], ident[:])
            for g in range(2):
                copy(eng, xgw[:, g, 0:R, n, :, :], xb[:, g, :, :].rearrange("p u (q r) -> p r q u", r=R))

        def shift():
            for g in range(2):
                nc.vector.tensor_copy(out=xgw[:, g, R:NPL, :, 0:31, :], in_=xgw[:, g, 0:3, :, 1:32, :])

        def quant_x(pl0, npl):
            c0 = pl0 * P
            w = npl * P
            for g in range(2):
                a = (g * HC + c0) * 4
                nc.vector.quantize_mx(out=xc[:, g, c0:c0 + w].bitcast(FP8X4), scales=xs[:, g, c0:c0 + w],
                                      in_=xg[:, a:a + 4 * w])

        def halve(h):
            nc.vector.tensor_copy(
                out=xch[h][:].bitcast(I32).rearrange("p g (r m) -> p (g r) m", r=NPL),
                in_=xc[:].bitcast(I32).rearrange("p g (r m) -> p (g r) m", r=NPL)[:, :, 64 * h:64 * h + 64])
            nc.vector.tensor_copy(
                out=xsh[h][:].rearrange("p g (r m) -> p (g r) m", r=NPL),
                in_=xs[:].rearrange("p g (r m) -> p (g r) m", r=NPL)[:, :, 64 * h:64 * h + 64])

        perm = {}
        turned = {}
        grp = {}
        cod = {}

        def permute(i, K, eng):
            if i < NI:
                pt = ppool.tile([P, K * D], BF16, name="p%d" % K, tag="p%d" % K)
                perm[(i, K)] = pt[:].bitcast(F32).rearrange("p (u w) -> p u w", u=2)
                copy(eng, perm[(i, K)], wraw[(i, K)][:].bitcast(F32).rearrange("p (w u) -> p u w", u=2))
                load_w(i + 3, K)

        def transposes(i, K):
            banks = []
            for k in range(K):
                bank = next_bank()[:].rearrange("p (g u f) -> p g u f", g=2, u=2)
                banks.append(bank)
                for g in range(2):
                    for u in range(2):
                        o = 256 * k + 128 * g
                        if (i, K) in perm:
                            words = perm[(i, K)][:, u, o:o + P]
                        else:
                            words = wraw[(i, K)][:].bitcast(F32)[:, 2 * o + u:2 * (o + P):2]
                        nc.tensor.transpose(bank[:, g, u, :], words, ident[:])
            turned[(i, K)] = banks

        def regroup(i, K, engs, k0=0):
            if (i, K) not in grp:
                grp[(i, K)] = gpool.tile([P, K * 1024], BF16, name="g%d" % K, tag="g%d" % K, align_bytes=64)
            gr_w = grp[(i, K)][:].bitcast(F32).rearrange("p (k g f u) -> p k g f u", k=K, g=2, f=P, u=2)
            for k in range(k0, k0 + len(engs)):
                if engs[k - k0] != "-":
                    copy(engs[k - k0], gr_w[:, k], turned[(i, K)][k].rearrange("p g u f -> p g f u"))

        def quantise(i, K):
            cw = cpool.tile([P, K * 256], U32, name="c%d" % K, tag="c%d" % K, align_bytes=64)
            sc = cpool.tile([P, K * 256], U8, name="s%d" % K, tag="s%d" % K, align_bytes=64)
            cod[(i, K)] = (cw, sc)
            gr = grp[(i, K)]
            for (a, w) in QCALLS[K]:
                nc.vector.quantize_mx(out=cw[:, a // 4:(a + w) // 4].bitcast(FP8X4),
                                      scales=sc[:, a // 4:(a + w) // 4], in_=gr[:, a:a + w])

        Tn = const.tile([P, NI, B * T], F32, name="Tn")
        ssum = const.tile([P, B * T], F32, name="ssum")
        rinv = const.tile([P, B * T], F32, name="rinv")
        O = const.tile([P, B, NI * (T - 1)], F32, name="O")
        accs = {}
        acc_tags = {}
        sums = ["s0", "s1"]
        for i in range(NI):
            for K in (ORDER if i > 0 else WIDTHS):
                if (i, K) not in OTHER_BANK:
                    acc_tags[(i, K)] = sums[0]
                    sums.reverse()
        sqs = {}
        rbs = {}

        def products(i, K, h):
            if h != 1:
                accs[(i, K)] = bank_of(acc_tags[(i, K)]) if (i, K) in acc_tags else next_bank()
            cw, sc = cod[(i, K)]
            if h is None:
                c, s, m, o = xc, xs, P, accs[(i, K)][:]
            else:
                c, s, m, o = xch[h], xsh[h], 64, accs[(i, K)][:, 256 * h:256 * h + 256]
            for k in range(K):
                for g in range(2):
                    j = (2 * k + g) * P
                    nc.tensor.matmul_mx(out=o, lhsT=cw[:, j:j + P].bitcast(FP8X4), lhsT_scale=sc[:, j:j + P],
                                        rhs=c[:, g, m * k:m * k + 4 * m].bitcast(FP8X4),
                                        rhs_scale=s[:, g, m * k:m * k + 4 * m],
                                        start=(k == 0 and g == 0), stop=(k == K - 1 and g == 1))

        def part(ap, h):
            return ap if h is None else ap[:, 256 * h:256 * h + 256]

        def relu(dst, i, K, h):
            nc.scalar.activation(out=dst.rearrange("p (m r) -> p m r", r=R),
                                 in_=part(accs[(i, K)][:], h).rearrange("p (r m) -> p m r", r=R),
                                 func=ACT.Relu, bias=bias[:, K - 2, i:i + 1])

        def first(i, h):
            relu(part(Tn[:, i], h), i, 4, h)

        def clear(eng, i, h, K):
            eng.memset(part(Tn[:, i], h).rearrange("p (n t) -> p n t", t=T)[:, :, T + 1 - K:T - 1], 0.0)

        def more(i, K, h):
            dst = part(Tn[:, i], h).rearrange("p (m r) -> p m r", r=R)
            nc.vector.scalar_tensor_tensor(
                out=dst, in0=part(accs[(i, K)][:], h).rearrange("p (r m) -> p m r", r=R),
                scalar=bias[:, K - 2, i:i + 1], in1=dst, op0=ALU.add, op1=ALU.max)

        def square(i, h):
            if i == 0:
                nc.scalar.activation(out=ssum[:], in_=Tn[:, 0], func=ACT.Square)
            else:
                sq = epool.tile([P, B * T if h is None else 256], F32, name="sq", tag="sq")
                sqs[(i, h)] = sq
                nc.scalar.activation(out=sq[:], in_=part(Tn[:, i], h), func=ACT.Square)

        def square_v(i, h):
            sq = epool.tile([P, 256], F32, name="sq", tag="sq")
            sqs[(i, h)] = sq
            t = Tn[:, i, 256 * h:256 * h + 256]
            nc.vector.tensor_tensor(out=sq[:], in0=t, in1=t, op=ALU.mult)

        def addsq(i, h):
            if i > 0:
                nc.vector.tensor_tensor(out=part(ssum[:], h), in0=part(ssum[:], h), in1=sqs[(i, h)][:], op=ALU.add)

        def norm(h, src, start, stop):
            if start:
                rbs[h] = next_bank()
            nc.tensor.matmul(out=rbs[h][:, 0:256], lhsT=ones[:], rhs=src, start=start, stop=stop)

        def rsqrt(h):
            nc.scalar.activation(out=rinv[:, 256 * h:256 * h + 256], in_=rbs[h][:, 0:256], func=ACT.Abs_reciprocal_sqrt)

        def scale(n, i0, i1):
            nc.vector.scalar_tensor_tensor(
                out=O[:, n, :].rearrange("p (i q) -> p i q", i=NI)[:, i0:i1, :],
                in0=rinv[:, T * n:T * n + T - 1].unsqueeze(1).to_broadcast([P, i1 - i0, T - 1]),
                scalar=1e12, in1=Tn[:, i0:i1, T * n:T * n + T - 1], op0=ALU.min, op1=ALU.mult)

        def store(n, c0, c1):
            nc.sync.dma_start(out=out[n].rearrange("(m i) q -> m (i q)", i=NI)[:, c0:c1], in_=O[:, n, c0:c1])

        def scale_store(n):
            scale(n, 0, NI)
            store(n, 0, NI * (T - 1))

        def busy(n):
            bank = next_bank()
            for r in range(n):
                nc.tensor.matmul(out=bank[:, 0:P], lhsT=ones[:], rhs=ones[:], start=True, stop=True)

        busy(5)
        tx(0, "V")
        tx(1, "S")
        tx(2, "V")
        tx(3, "S")
        busy(1)
        quant_x(0, 4)
        transposes(0, 2)
        regroup(0, 2, "SS")
        busy(1)
        shift()
        quant_x(4, 2)
        quantise(0, 2)
        quant_x(6, 1)
        transposes(0, 3)
        regroup(0, 3, "SSS")
        busy(2)
        products(0, 2, None)
        permute(0, 4, "V")
        quantise(0, 3)
        for K in WIDTHS:
            nc.vector.tensor_copy(out=bias[:, K - 2, :], in_=braw[K][:])
        transposes(0, 4)
        t2 = epool.tile([P, B * T], F32, name="t2", tag="sq")
        regroup(0, 4, "SSSS")
        relu(t2[:], 0, 2, None)
        load_w(3, 3)
        load_w(3, 2)
        permute(1, 4, "V")
        products(0, 3, None)
        permute(1, 3, "V")
        quantise(0, 4)
        permute(1, 2, "V")
        transposes(1, 4)
        regroup(1, 4, "SSSV")
        permute(2, 4, "V")
        transposes(1, 3)
        regroup(1, 3, "SSS")
        quantise(1, 4)
        permute(2, 3, "V")
        transposes(1, 2)
        regroup(1, 2, "SS")
        permute(2, 2, "V")
        products(0, 4, None)
        first(0, None)
        clear(nc.gpsimd, 0, None, 4)
        quantise(1, 3)
        more(0, 3, None)
        clear(nc.gpsimd, 0, None, 3)
        quantise(1, 2)
        for s in range(1, NI - 1):
            j = s + 1
            transposes(j, 4)
            regroup(j, 4, "SSSS" if s == 1 else "S-SS")
            if s > 1:
                clear(nc.gpsimd, s - 1, None, 4)
                more(s - 1, 3, None)
                clear(nc.gpsimd, s - 1, None, 3)
                regroup(j, 4, "V", 1)
                if s > 2:
                    permute(s + 2, 4, "V")
                more(s - 1, 2, None)
            else:
                nc.vector.tensor_tensor(out=Tn[:, 0], in0=Tn[:, 0], in1=t2[:], op=ALU.max)
            transposes(j, 3)
            regroup(j, 3, "SSS")
            quantise(j, 4)
            if s <= 2:
                permute(s + 2, 4, "V")
            quantise(j, 3)
            transposes(j, 2)
            permute(s + 2, 3, "V")
            if s < NI - 2:
                regroup(j, 2, "SS")
                quantise(j, 2)
                products(s, 4, None)
                first(s, None)
                square(s - 1, None)
                permute(s + 2, 2, "S")
                addsq(s - 1, None)
                products(s, 3, None)
                products(s, 2, None)
                if s in (2, 4):
                    halve(s // 2 - 1)
        a = NI - 2
        b = NI - 1
        products(a, 4, 0)
        first(a, 0)
        regroup(b, 2, "SS")
        square(a - 1, None)
        products(a, 3, 0)
        clear(nc.vector, a, 0, 4)
        more(a, 3, 0)
        clear(nc.vector, a, 0, 3)
        quantise(b, 2)
        addsq(a - 1, None)
        products(a, 2, 0)
        more(a, 2, 0)
        products(b, 4, 0)
        first(b, 0)
        square(a, 0)
        clear(nc.vector, b, 0, 4)
        products(b, 3, 0)
        more(b, 3, 0)
        addsq(a, 0)
        clear(nc.vector, b, 0, 3)
        products(b, 2, 0)
        more(b, 2, 0)
        square_v(b, 0)
        products(a, 4, 1)
        first(a, 1)
        addsq(b, 0)
        products(a, 3, 1)
        clear(nc.vector, a, 1, 4)
        more(a, 3, 1)
        clear(nc.vector, a, 1, 3)
        products(a, 2, 1)
        norm(0, ssum[:, 0:256], True, True)
        rsqrt(0)
        more(a, 2, 1)
        square(a, 1)
        products(b, 4, 1)
        first(b, 1)
        scale_store(0)
        addsq(a, 1)
        clear(nc.vector, b, 1, 4)
        products(b, 3, 1)
        more(b, 3, 1)
        clear(nc.vector, b, 1, 3)
        products(b, 2, 1)
        norm(1, ssum[:, 256:512], True, False)
        more(b, 2, 1)
        square_v(b, 1)
        norm(1, sqs[(b, 1)][:], False, True)
        scale_store(1)
        rsqrt(1)
        for n in (2, 3):
            scale(n, 0, 5)
            store(n, 0, 608)
            scale(n, 5, NI)
            store(n, 608, NI * (T - 1))
